import numpy as np
import ml_dtypes


def mxq(x, axis, fmt="e4m3"):
    dtype, down = {"e4m3": (ml_dtypes.float8_e4m3fn, 7), "e5m2": (ml_dtypes.float8_e5m2, 14)}[fmt]
    v = np.moveaxis(np.asarray(x, np.float32).astype(ml_dtypes.bfloat16).astype(np.float64), axis, -1)
    blocks = v.reshape(v.shape[:-1] + (-1, 32))
    amax = np.abs(blocks).max(-1, keepdims=True)
    byte = np.maximum(np.where(amax > 0, np.frexp(amax)[1] - 1 + 127, 0) - down, 1)
    scale = np.exp2(byte - 127.0)
    codes = (blocks / scale).astype(np.float32).astype(dtype).astype(np.float64)
    return np.moveaxis((codes * scale).reshape(v.shape), -1, axis)


WIDE = False


def mx_kscale(k):
    if not WIDE:
        return np.ones(k)
    levels = np.array([10, -10, 5, -5, 0])
    a = np.random.permutation(np.resize(levels, k // 512 * 4)).reshape(k // 512, 4)
    idx = np.arange(k)
    return np.exp2(a[idx // 512, idx % 128 // 32])


BF16 = ml_dtypes.bfloat16


def bf(x):
    return np.asarray(x, np.float32).astype(BF16)


def f64(x):
    return np.asarray(x).astype(np.float64)


E2M1 = np.array([0.0, 0.5, 1.0, 1.5, 2.0, 3.0, 4.0, 6.0, -0.0, -0.5, -1.0, -1.5, -2.0, -3.0, -4.0, -6.0])


def pack_weight(w, fmt):
    k, n = w.shape
    w = f64(bf(w)).reshape(k // 32, 32, n)
    amax = np.abs(w).max(1)
    if fmt == "e4m3":
        byte = np.frexp(amax)[1] - 1 + 127 - 7
    else:
        mant, ex = np.frexp(amax / 6.0)
        byte = np.where(mant > 0.5, ex, ex - 1) + 127
    byte = np.clip(np.where(amax > 0, byte, 1), 1, 254)
    scaled = (w * np.exp2(127.0 - byte)[:, None, :]).reshape(k, n).astype(np.float32)
    by_word = np.ascontiguousarray(scaled.reshape(k // 512, 128, 4, n).transpose(0, 1, 3, 2))
    if fmt == "e4m3":
        words = by_word.astype(ml_dtypes.float8_e4m3fn).view(np.uint8)
    else:
        c = by_word.astype(ml_dtypes.float4_e2m1fn).view(np.uint8) & 0xF
        words = c[..., 0::2] | (c[..., 1::2] << 4)
    return np.ascontiguousarray(words), np.ascontiguousarray(byte.astype(np.uint8).reshape(k // 512, 16, n))


def unpack_weight(words, scales, fmt):
    g, p, n, _ = words.shape
    if fmt == "e4m3":
        vals = np.ascontiguousarray(words).view(ml_dtypes.float8_e4m3fn).astype(np.float64)
    else:
        nib = np.empty((g, p, n, 4), np.uint8)
        nib[..., 0::2] = words & 0xF
        nib[..., 1::2] = words >> 4
        vals = E2M1[nib]
    vals = vals * np.repeat(np.exp2(scales.astype(np.float64) - 127.0), 8, axis=1)[..., None]
    return vals.transpose(0, 1, 3, 2).reshape(g * 512, n)


B, D_IN, D_H = 512, 1024, 1024
FMT = "e4m3"


def sigmoid(v):
    return 1.0 / (1.0 + np.exp(-v))


def setup_inputs():
    s, t = mx_kscale(D_IN), mx_kscale(D_H)

    def w_in():
        return pack_weight(np.ascontiguousarray((np.random.standard_normal((D_H, D_IN)) * 0.6 / np.sqrt(D_IN) / s[None, :]).T), FMT)

    def w_rec():
        return pack_weight(np.ascontiguousarray((np.random.standard_normal((D_H, D_H)) * 0.6 / np.sqrt(D_H) / t[None, :]).T), FMT)

    def bias():
        return bf(np.random.standard_normal(D_H) * 0.3)

    incoming = bf(np.random.standard_normal((B, D_IN)) * s)
    h = bf(np.random.standard_normal((B, D_H)) * t)
    W_i_words, W_i_scales = w_in()
    b_W_i = bias()
    W_c_words, W_c_scales = w_in()
    b_W_c = bias()
    U_i_words, U_i_scales = w_rec()
    b_U_i = bias()
    U_c_words, U_c_scales = w_rec()
    b_U_c = bias()
    return {"incoming": incoming, "h": h,
            "W_i_words": W_i_words, "W_i_scales": W_i_scales, "b_W_i": b_W_i,
            "W_c_words": W_c_words, "W_c_scales": W_c_scales, "b_W_c": b_W_c,
            "U_i_words": U_i_words, "U_i_scales": U_i_scales, "b_U_i": b_U_i,
            "U_c_words": U_c_words, "U_c_scales": U_c_scales, "b_U_c": b_U_c}


def reference(incoming, h, W_i_words, W_i_scales, b_W_i, W_c_words, W_c_scales, b_W_c, U_i_words, U_i_scales, b_U_i, U_c_words, U_c_scales, b_U_c):
    xq = mxq(f64(incoming), 1, "e4m3")
    hq = mxq(f64(h), 1, "e4m3")
    I = sigmoid((xq @ unpack_weight(W_i_words, W_i_scales, FMT)) + f64(b_W_i) + (hq @ unpack_weight(U_i_words, U_i_scales, FMT)) + f64(b_U_i))
    C_head = (xq @ unpack_weight(W_c_words, W_c_scales, FMT)) + f64(b_W_c) + (hq @ unpack_weight(U_c_words, U_c_scales, FMT)) + f64(b_U_c)
    return I * C_head

@@ -1,0 +1,165 @@
+from contextlib import ExitStack
+
+import concourse.mybir as mybir
+from concourse.masks import make_identity
+
+F32 = mybir.dt.float32
+BF16 = mybir.dt.bfloat16
+I32 = mybir.dt.int32
+U32 = mybir.dt.uint32
+U8 = mybir.dt.uint8
+FP8X4 = mybir.dt.float8_e4m3fn_x4
+ADD = mybir.AluOpType.add
+MULT = mybir.AluOpType.mult
+SIGMOID = mybir.ActivationFunctionType.Sigmoid
+
+P = 128
+PACK = 4
+K_PASS = P * PACK
+BATCH = 512
+D_IN = 1024
+D_OUT = 1024
+ROW_TILES = BATCH // P
+PASSES = D_IN // K_PASS
+N_TILE = 512
+COL_TILES = D_OUT // N_TILE
+QUADRANTS = 4
+ROWS_PER_QUADRANT = 4
+SOURCES = 2
+GATES = 2
+INPUT_GATE = 0
+
+FLOPS = 2 * BATCH * (SOURCES * D_IN) * (GATES * D_OUT)
+
+
+def tile_lstmcell_pa_kernel(
+    tc,
+    incoming, h,
+    W_i_words, W_i_scales, b_W_i,
+    W_c_words, W_c_scales, b_W_c,
+    U_i_words, U_i_scales, b_U_i,
+    U_c_words, U_c_scales, b_U_c,
+    out,
+):
+    nc = tc.nc
+    words_dram = [[W_i_words, U_i_words], [W_c_words, U_c_words]]
+    scales_dram = [[W_i_scales, U_i_scales], [W_c_scales, U_c_scales]]
+    bias_dram = [[b_W_i, b_U_i], [b_W_c, b_U_c]]
+    acts_dram = [a.rearrange("(p t) k -> p t k", t=ROW_TILES) for a in (incoming, h)]
+    out_rows = out.rearrange("(p t) n -> p t n", t=ROW_TILES)
+
+    with ExitStack() as ctx:
+        keep = ctx.enter_context(tc.tile_pool(name="keep", bufs=1))
+        stage = ctx.enter_context(tc.tile_pool(name="stage", bufs=3))
+        gates = ctx.enter_context(tc.tile_pool(name="gates", bufs=2 * ROW_TILES))
+        results = ctx.enter_context(tc.tile_pool(name="results", bufs=ROW_TILES))
+        psum = ctx.enter_context(tc.psum_pool(name="psum", bufs=8))
+        ctx.enter_context(tc.manual_schedule())
+
+        w_scales = keep.tile([P, GATES, D_OUT], U8, align_bytes=64)
+        nc.vector.memset(w_scales[:].rearrange("p a n -> p (a n)").bitcast(I32), 0)
+        bias_rows = keep.tile([P, GATES, D_OUT], BF16)
+        nc.vector.memset(bias_rows[:], 0.0)
+        ones = keep.tile([P, P], BF16)
+        nc.vector.memset(ones[:], 1.0)
+        warm = keep.tile([P, 1], F32)
+        nc.vector.memset(warm[:], 0.0)
+        nc.scalar.activation(out=warm[:], in_=warm[:], func=SIGMOID)
+        ident = keep.tile([P, P], F32)
+        make_identity(nc, ident[:])
+        for gate in range(GATES):
+            for source in range(SOURCES):
+                nc.gpsimd.dma_start(
+                    out=bias_rows[source : source + 1, gate, :],
+                    in_=bias_dram[gate][source].rearrange("(o n) -> o n", o=1),
+                )
+
+        def load_scale_rows(gate, quadrant):
+            rows = slice(ROWS_PER_QUADRANT * quadrant, ROWS_PER_QUADRANT * (quadrant + 1))
+            for source in range(SOURCES):
+                first = 32 * quadrant + ROWS_PER_QUADRANT * PASSES * source
+                nc.sync.dma_start(
+                    out=w_scales[first : first + ROWS_PER_QUADRANT * PASSES, gate, :].bitcast(I32),
+                    in_=scales_dram[gate][source][:, rows, :].bitcast(I32),
+                )
+
+        act_raw = [keep.tile([P, ROW_TILES, D_IN], BF16, name="act_raw%d" % s) for s in range(SOURCES)]
+        for source in range(SOURCES):
+            for half in range(2):
+                tiles = slice(2 * half, 2 * half + 2)
+                nc.sync.dma_start(out=act_raw[source][:, tiles, :], in_=acts_dram[source][:, tiles, :])
+                load_scale_rows(INPUT_GATE, 2 * source + half)
+        w_words = {}
+        for col in range(COL_TILES):
+            for gate in range(GATES):
+                for source in range(SOURCES):
+                    chunk = keep.tile([P, PASSES, N_TILE], U32, name="w%d%d%d" % (col, gate, source), align_bytes=64)
+                    w_words[(col, gate, source)] = chunk
+                    view = words_dram[gate][source].rearrange("g p n t -> p g (n t)")
+                    nc.sync.dma_start(
+                        out=chunk[:].bitcast(I32),
+                        in_=view[:, :, PACK * N_TILE * col : PACK * N_TILE * (col + 1)].bitcast(I32),
+                    )
+                    if col == 0:
+                        load_scale_rows(1 - INPUT_GATE, 2 * gate + source)
+
+        act_codes = keep.tile([P, SOURCES, ROW_TILES, PASSES * P], U32, align_bytes=64)
+        act_scales = keep.tile([P, SOURCES, ROW_TILES, PASSES * P], U8, align_bytes=64)
+        for source in range(SOURCES):
+            for t in range(ROW_TILES):
+                pairs = act_raw[source][:, t, :].bitcast(F32)
+                flipped = psum.tile([P, PASSES, 2, P], F32, tag="bank")
+                for g in range(PASSES):
+                    for u in range(2):
+                        nc.tensor.transpose(
+                            flipped[:, g, u, :],
+                            pairs[:, (K_PASS // 2) * g + u : (K_PASS // 2) * (g + 1) : 2],
+                            ident[:],
+                        )
+                grouped = stage.tile([P, PASSES * P * PACK], BF16, align_bytes=64)
+                nc.scalar.copy(
+                    out=grouped[:].bitcast(F32).rearrange("p (g b u) -> p g b u", g=PASSES, u=2),
+                    in_=flipped[:].rearrange("p g u b -> p g b u"),
+                )
+                nc.vector.quantize_mx(
+                    out=act_codes[:, source, t, :].bitcast(FP8X4),
+                    scales=act_scales[:, source, t, :],
+                    in_=grouped[:],
+                )
+
+        bias = keep.tile([P, GATES, D_OUT], F32)
+        for col in range(COL_TILES):
+            cols = slice(N_TILE * col, N_TILE * (col + 1))
+            for gate in range(GATES):
+                spread = psum.tile([P, N_TILE], F32, tag="bank")
+                nc.tensor.matmul(out=spread[:], lhsT=ones[:], rhs=bias_rows[:, gate, cols], start=True, stop=True)
+                nc.scalar.copy(out=bias[:, gate, cols], in_=spread[:])
+
+        for col in range(COL_TILES):
+            cols = slice(N_TILE * col, N_TILE * (col + 1))
+            input_gate = []
+            for gate in range(GATES):
+                for t in range(ROW_TILES):
+                    acc = psum.tile([P, N_TILE], F32, tag="bank")
+                    for source in range(SOURCES):
+                        for g in range(PASSES):
+                            offset = ROWS_PER_QUADRANT * (PASSES * source + g)
+                            nc.tensor.matmul_mx(
+                                out=acc[:],
+                                lhsT=act_codes[:, source, t, P * g : P * (g + 1)].bitcast(FP8X4),
+                                lhsT_scale=act_scales[:, source, t, P * g : P * (g + 1)],
+                                rhs=w_words[(col, gate, source)][:, g, :].bitcast(FP8X4),
+                                rhs_scale=w_scales[offset:P, gate, cols],
+                                start=(source == 0 and g == 0),
+                                stop=(source == SOURCES - 1 and g == PASSES - 1),
+                            )
+                    if gate == INPUT_GATE:
+                        opened = gates.tile([P, N_TILE], F32)
+                        nc.vector.tensor_tensor(out=opened[:], in0=acc[:], in1=bias[:, gate, cols], op=ADD)
+                        nc.scalar.activation(out=opened[:], in_=opened[:], func=SIGMOID)
+                        input_gate.append(opened)
+                    else:
+                        result = results.tile([P, N_TILE], F32)
+                        nc.vector.tensor_tensor(out=result[:], in0=acc[:], in1=bias[:, gate, cols], op=ADD)
+                        nc.vector.tensor_tensor(out=result[:], in0=result[:], in1=input_gate[t][:], op=MULT)
+                        nc.sync.dma_start(out=out_rows[:, t, cols], in_=result[:])

@@ -56,58 +56,72 @@ def tile_lstmcell_pa_kernel(
         psum = ctx.enter_context(tc.psum_pool(name="psum", bufs=8))
         ctx.enter_context(tc.manual_schedule())
 
-        w_scales = keep.tile([P, GATES, D_OUT], U8, align_bytes=64)
-        nc.vector.memset(w_scales[:].rearrange("p a n -> p (a n)").bitcast(I32), 0)
+        w_scales = [keep.tile([P, D_OUT], U8, name="w_scales%d" % gate, align_bytes=64) for gate in range(GATES)]
+        nc.vector.memset(w_scales[INPUT_GATE][:].bitcast(I32), 0)
         bias_rows = keep.tile([P, GATES, D_OUT], BF16)
         nc.vector.memset(bias_rows[:], 0.0)
+        nc.vector.memset(w_scales[1 - INPUT_GATE][:].bitcast(I32), 0)
         ones = keep.tile([P, P], BF16)
         nc.vector.memset(ones[:], 1.0)
         warm = keep.tile([P, 1], F32)
-        nc.vector.memset(warm[:], 0.0)
+        nc.gpsimd.memset(warm[:], 0.0)
         nc.scalar.activation(out=warm[:], in_=warm[:], func=SIGMOID)
         ident = keep.tile([P, P], F32)
         make_identity(nc, ident[:])
         for gate in range(GATES):
             for source in range(SOURCES):
-                nc.gpsimd.dma_start(
+                nc.scalar.dma_start(
                     out=bias_rows[source : source + 1, gate, :],
                     in_=bias_dram[gate][source].rearrange("(o n) -> o n", o=1),
                 )
 
-        def load_scale_rows(gate, quadrant):
-            rows = slice(ROWS_PER_QUADRANT * quadrant, ROWS_PER_QUADRANT * (quadrant + 1))
-            for source in range(SOURCES):
-                first = 32 * quadrant + ROWS_PER_QUADRANT * PASSES * source
-                nc.sync.dma_start(
-                    out=w_scales[first : first + ROWS_PER_QUADRANT * PASSES, gate, :].bitcast(I32),
-                    in_=scales_dram[gate][source][:, rows, :].bitcast(I32),
-                )
-
-        act_raw = [keep.tile([P, ROW_TILES, D_IN], BF16, name="act_raw%d" % s) for s in range(SOURCES)]
-        for source in range(SOURCES):
-            for half in range(2):
-                tiles = slice(2 * half, 2 * half + 2)
-                nc.sync.dma_start(out=act_raw[source][:, tiles, :], in_=acts_dram[source][:, tiles, :])
-                load_scale_rows(INPUT_GATE, 2 * source + half)
-        w_words = {}
-        for col in range(COL_TILES):
-            for gate in range(GATES):
+        def load_scales(gate):
+            for quadrant in range(QUADRANTS):
+                rows = slice(ROWS_PER_QUADRANT * quadrant, ROWS_PER_QUADRANT * (quadrant + 1))
                 for source in range(SOURCES):
-                    chunk = keep.tile([P, PASSES, N_TILE], U32, name="w%d%d%d" % (col, gate, source), align_bytes=64)
-                    w_words[(col, gate, source)] = chunk
-                    view = words_dram[gate][source].rearrange("g p n t -> p g (n t)")
+                    first = 32 * quadrant + ROWS_PER_QUADRANT * PASSES * source
                     nc.sync.dma_start(
-                        out=chunk[:].bitcast(I32),
-                        in_=view[:, :, PACK * N_TILE * col : PACK * N_TILE * (col + 1)].bitcast(I32),
+                        out=w_scales[gate][first : first + ROWS_PER_QUADRANT * PASSES, :].bitcast(I32),
+                        in_=scales_dram[gate][source][:, rows, :].bitcast(I32),
                     )
-                    if col == 0:
-                        load_scale_rows(1 - INPUT_GATE, 2 * gate + source)
 
-        act_codes = keep.tile([P, SOURCES, ROW_TILES, PASSES * P], U32, align_bytes=64)
-        act_scales = keep.tile([P, SOURCES, ROW_TILES, PASSES * P], U8, align_bytes=64)
+        w_words = {}
+
+        def load_words(col, gate, source):
+            chunk = keep.tile([P, PASSES, N_TILE], U32, name="w%d%d%d" % (col, gate, source), align_bytes=64)
+            w_words[(col, gate, source)] = chunk
+            view = words_dram[gate][source].rearrange("g p n t -> p g (n t)")
+            nc.sync.dma_start(
+                out=chunk[:].bitcast(I32),
+                in_=view[:, :, PACK * N_TILE * col : PACK * N_TILE * (col + 1)].bitcast(I32),
+            )
+
+        act_raw = [
+            [keep.tile([P, D_IN], BF16, name="act_raw%d%d" % (s, t)) for t in range(ROW_TILES)]
+            for s in range(SOURCES)
+        ]
         for source in range(SOURCES):
             for t in range(ROW_TILES):
-                pairs = act_raw[source][:, t, :].bitcast(F32)
+                nc.sync.dma_start(out=act_raw[source][t][:], in_=acts_dram[source][:, t, :])
+        for col in range(COL_TILES):
+            for gate in range(GATES):
+                if col == 0:
+                    load_scales(gate)
+                for source in range(SOURCES):
+                    load_words(col, gate, source)
+
+        act_codes = [
+            [keep.tile([P, PASSES * P], U32, name="codes%d%d" % (s, t), align_bytes=64) for t in range(ROW_TILES)]
+            for s in range(SOURCES)
+        ]
+        act_scales = [
+            [keep.tile([P, PASSES * P], U8, name="scales%d%d" % (s, t), align_bytes=64) for t in range(ROW_TILES)]
+            for s in range(SOURCES)
+        ]
+
+        def turn_and_quantise(source):
+            for t in range(ROW_TILES):
+                pairs = act_raw[source][t][:].bitcast(F32)
                 flipped = psum.tile([P, PASSES, 2, P], F32, tag="bank")
                 for g in range(PASSES):
                     for u in range(2):
@@ -122,44 +136,78 @@ def tile_lstmcell_pa_kernel(
                     in_=flipped[:].rearrange("p g u b -> p g b u"),
                 )
                 nc.vector.quantize_mx(
-                    out=act_codes[:, source, t, :].bitcast(FP8X4),
-                    scales=act_scales[:, source, t, :],
+                    out=act_codes[source][t][:].bitcast(FP8X4),
+                    scales=act_scales[source][t][:],
                     in_=grouped[:],
                 )
 
+        turn_and_quantise(0)
+
         bias = keep.tile([P, GATES, D_OUT], F32)
-        for col in range(COL_TILES):
-            cols = slice(N_TILE * col, N_TILE * (col + 1))
-            for gate in range(GATES):
+        for gate in range(GATES):
+            for col in range(COL_TILES):
+                cols = slice(N_TILE * col, N_TILE * (col + 1))
                 spread = psum.tile([P, N_TILE], F32, tag="bank")
                 nc.tensor.matmul(out=spread[:], lhsT=ones[:], rhs=bias_rows[:, gate, cols], start=True, stop=True)
-                nc.scalar.copy(out=bias[:, gate, cols], in_=spread[:])
+                nc.vector.tensor_copy(out=bias[:, gate, cols], in_=spread[:])
 
-        for col in range(COL_TILES):
+        turn_and_quantise(1)
+
+        accs = {}
+        input_gate = {}
+        sums = {}
+
+        def passes(col, gate, t, source):
+            if source == 0:
+                accs[(col, gate, t)] = psum.tile([P, N_TILE], F32, tag="bank", name="acc")
             cols = slice(N_TILE * col, N_TILE * (col + 1))
-            input_gate = []
-            for gate in range(GATES):
-                for t in range(ROW_TILES):
-                    acc = psum.tile([P, N_TILE], F32, tag="bank")
-                    for source in range(SOURCES):
-                        for g in range(PASSES):
-                            offset = ROWS_PER_QUADRANT * (PASSES * source + g)
-                            nc.tensor.matmul_mx(
-                                out=acc[:],
-                                lhsT=act_codes[:, source, t, P * g : P * (g + 1)].bitcast(FP8X4),
-                                lhsT_scale=act_scales[:, source, t, P * g : P * (g + 1)],
-                                rhs=w_words[(col, gate, source)][:, g, :].bitcast(FP8X4),
-                                rhs_scale=w_scales[offset:P, gate, cols],
-                                start=(source == 0 and g == 0),
-                                stop=(source == SOURCES - 1 and g == PASSES - 1),
-                            )
-                    if gate == INPUT_GATE:
-                        opened = gates.tile([P, N_TILE], F32)
-                        nc.vector.tensor_tensor(out=opened[:], in0=acc[:], in1=bias[:, gate, cols], op=ADD)
-                        nc.scalar.activation(out=opened[:], in_=opened[:], func=SIGMOID)
-                        input_gate.append(opened)
-                    else:
-                        result = results.tile([P, N_TILE], F32)
-                        nc.vector.tensor_tensor(out=result[:], in0=acc[:], in1=bias[:, gate, cols], op=ADD)
-                        nc.vector.tensor_tensor(out=result[:], in0=result[:], in1=input_gate[t][:], op=MULT)
-                        nc.sync.dma_start(out=out_rows[:, t, cols], in_=result[:])
+            for g in range(PASSES):
+                offset = ROWS_PER_QUADRANT * (PASSES * source + g)
+                nc.tensor.matmul_mx(
+                    out=accs[(col, gate, t)][:],
+                    lhsT=act_codes[source][t][:, P * g : P * (g + 1)].bitcast(FP8X4),
+                    lhsT_scale=act_scales[source][t][:, P * g : P * (g + 1)],
+                    rhs=w_words[(col, gate, source)][:, g, :].bitcast(FP8X4),
+                    rhs_scale=w_scales[gate][offset:P, cols],
+                    start=(source == 0 and g == 0),
+                    stop=(source == SOURCES - 1 and g == PASSES - 1),
+                )
+
+        def add_bias(col, gate, t):
+            cols = slice(N_TILE * col, N_TILE * (col + 1))
+            if gate == INPUT_GATE:
+                opened = gates.tile([P, N_TILE], F32)
+                nc.vector.tensor_tensor(out=opened[:], in0=accs[(col, gate, t)][:], in1=bias[:, gate, cols], op=ADD)
+                nc.scalar.activation(out=opened[:], in_=opened[:], func=SIGMOID)
+                input_gate[(col, t)] = opened
+            else:
+                result = results.tile([P, N_TILE], F32)
+                nc.vector.tensor_tensor(out=result[:], in0=accs[(col, gate, t)][:], in1=bias[:, gate, cols], op=ADD)
+                sums[(col, t)] = result
+
+        def finish(col, t):
+            cols = slice(N_TILE * col, N_TILE * (col + 1))
+            result = sums[(col, t)]
+            nc.vector.tensor_tensor(out=result[:], in0=result[:], in1=input_gate[(col, t)][:], op=MULT)
+            nc.sync.dma_start(out=out_rows[:, t, cols], in_=result[:])
+
+        for source in range(SOURCES):
+            for t in range(ROW_TILES):
+                passes(0, INPUT_GATE, t, source)
+                if source == SOURCES - 1:
+                    add_bias(0, INPUT_GATE, t)
+        order = [
+            (0, 1, 0), (0, 1, 1), (0, 1, 2), (1, 0, 0), (0, 1, 3), (1, 0, 1),
+            (1, 1, 0), (1, 0, 2), (1, 1, 1), (1, 0, 3), (1, 1, 2), (1, 1, 3),
+        ]
+        waiting = None
+        for col, gate, t in order:
+            for source in range(SOURCES):
+                passes(col, gate, t, source)
+            add_bias(col, gate, t)
+            if waiting is not None:
+                finish(waiting[0], waiting[1])
+                waiting = None
+            if gate != INPUT_GATE:
+                waiting = (col, t)
+        finish(waiting[0], waiting[1])

@@ -56,11 +56,18 @@ def tile_lstmcell_pa_kernel(
         psum = ctx.enter_context(tc.psum_pool(name="psum", bufs=8))
         ctx.enter_context(tc.manual_schedule())
 
-        w_scales = [keep.tile([P, D_OUT], U8, name="w_scales%d" % gate, align_bytes=64) for gate in range(GATES)]
-        nc.vector.memset(w_scales[INPUT_GATE][:].bitcast(I32), 0)
+        w_scales = {}
+        for gate in range(GATES):
+            for source in range(SOURCES):
+                w_scales[(gate, source)] = keep.tile(
+                    [P, D_OUT], U8, name="w_scales%d%d" % (gate, source), align_bytes=64
+                )
+        nc.vector.memset(w_scales[(INPUT_GATE, 0)][:].bitcast(I32), 0)
         bias_rows = keep.tile([P, GATES, D_OUT], BF16)
         nc.vector.memset(bias_rows[:], 0.0)
-        nc.vector.memset(w_scales[1 - INPUT_GATE][:].bitcast(I32), 0)
+        nc.vector.memset(w_scales[(INPUT_GATE, 1)][:].bitcast(I32), 0)
+        nc.vector.memset(w_scales[(1 - INPUT_GATE, 0)][:].bitcast(I32), 0)
+        nc.vector.memset(w_scales[(1 - INPUT_GATE, 1)][:].bitcast(I32), 0)
         ones = keep.tile([P, P], BF16)
         nc.vector.memset(ones[:], 1.0)
         warm = keep.tile([P, 1], F32)
@@ -75,15 +82,14 @@ def tile_lstmcell_pa_kernel(
                     in_=bias_dram[gate][source].rearrange("(o n) -> o n", o=1),
                 )
 
-        def load_scales(gate):
+        def load_scales(gate, source):
             for quadrant in range(QUADRANTS):
                 rows = slice(ROWS_PER_QUADRANT * quadrant, ROWS_PER_QUADRANT * (quadrant + 1))
-                for source in range(SOURCES):
-                    first = 32 * quadrant + ROWS_PER_QUADRANT * PASSES * source
-                    nc.sync.dma_start(
-                        out=w_scales[gate][first : first + ROWS_PER_QUADRANT * PASSES, :].bitcast(I32),
-                        in_=scales_dram[gate][source][:, rows, :].bitcast(I32),
-                    )
+                first = 32 * quadrant
+                nc.sync.dma_start(
+                    out=w_scales[(gate, source)][first : first + ROWS_PER_QUADRANT * PASSES, :].bitcast(I32),
+                    in_=scales_dram[gate][source][:, rows, :].bitcast(I32),
+                )
 
         w_words = {}
 
@@ -100,15 +106,23 @@ def tile_lstmcell_pa_kernel(
             [keep.tile([P, D_IN], BF16, name="act_raw%d%d" % (s, t)) for t in range(ROW_TILES)]
             for s in range(SOURCES)
         ]
-        for source in range(SOURCES):
+        def load_tiles(source):
             for t in range(ROW_TILES):
                 nc.sync.dma_start(out=act_raw[source][t][:], in_=acts_dram[source][:, t, :])
-        for col in range(COL_TILES):
-            for gate in range(GATES):
-                if col == 0:
-                    load_scales(gate)
-                for source in range(SOURCES):
-                    load_words(col, gate, source)
+
+        load_tiles(0)
+        load_scales(INPUT_GATE, 0)
+        load_tiles(1)
+        load_words(0, INPUT_GATE, 0)
+        load_scales(INPUT_GATE, 1)
+        load_words(0, INPUT_GATE, 1)
+        load_scales(1 - INPUT_GATE, 0)
+        load_words(0, 1 - INPUT_GATE, 0)
+        load_scales(1 - INPUT_GATE, 1)
+        load_words(0, 1 - INPUT_GATE, 1)
+        for gate in range(GATES):
+            for source in range(SOURCES):
+                load_words(1, gate, source)
 
         act_codes = [
             [keep.tile([P, PASSES * P], U32, name="codes%d%d" % (s, t), align_bytes=64) for t in range(ROW_TILES)]
@@ -162,13 +176,12 @@ def tile_lstmcell_pa_kernel(
                 accs[(col, gate, t)] = psum.tile([P, N_TILE], F32, tag="bank", name="acc")
             cols = slice(N_TILE * col, N_TILE * (col + 1))
             for g in range(PASSES):
-                offset = ROWS_PER_QUADRANT * (PASSES * source + g)
                 nc.tensor.matmul_mx(
                     out=accs[(col, gate, t)][:],
                     lhsT=act_codes[source][t][:, P * g : P * (g + 1)].bitcast(FP8X4),
                     lhsT_scale=act_scales[source][t][:, P * g : P * (g + 1)],
                     rhs=w_words[(col, gate, source)][:, g, :].bitcast(FP8X4),
-                    rhs_scale=w_scales[gate][offset:P, cols],
+                    rhs_scale=w_scales[(gate, source)][ROWS_PER_QUADRANT * g : P, cols],
                     start=(source == 0 and g == 0),
                     stop=(source == SOURCES - 1 and g == PASSES - 1),
                 )

@@ -171,38 +171,45 @@ def tile_lstmcell_pa_kernel(
         input_gate = {}
         sums = {}
 
-        def passes(col, gate, t, source):
+        def passes(col, gate, t, source, first=0, width=N_TILE):
+            key = (col, gate, t, first)
             if source == 0:
-                accs[(col, gate, t)] = psum.tile([P, N_TILE], F32, tag="bank", name="acc")
-            cols = slice(N_TILE * col, N_TILE * (col + 1))
+                accs[key] = psum.tile([P, width], F32, tag="bank", name="acc")
+            cols = slice(N_TILE * col + first, N_TILE * col + first + width)
             for g in range(PASSES):
                 nc.tensor.matmul_mx(
-                    out=accs[(col, gate, t)][:],
+                    out=accs[key][:],
                     lhsT=act_codes[source][t][:, P * g : P * (g + 1)].bitcast(FP8X4),
                     lhsT_scale=act_scales[source][t][:, P * g : P * (g + 1)],
-                    rhs=w_words[(col, gate, source)][:, g, :].bitcast(FP8X4),
+                    rhs=w_words[(col, gate, source)][:, g, first : first + width].bitcast(FP8X4),
                     rhs_scale=w_scales[(gate, source)][ROWS_PER_QUADRANT * g : P, cols],
                     start=(source == 0 and g == 0),
                     stop=(source == SOURCES - 1 and g == PASSES - 1),
                 )
 
-        def add_bias(col, gate, t):
-            cols = slice(N_TILE * col, N_TILE * (col + 1))
+        def add_bias(col, gate, t, first=0, width=N_TILE):
+            cols = slice(N_TILE * col + first, N_TILE * col + first + width)
+            acc = accs[(col, gate, t, first)]
             if gate == INPUT_GATE:
                 opened = gates.tile([P, N_TILE], F32)
-                nc.vector.tensor_tensor(out=opened[:], in0=accs[(col, gate, t)][:], in1=bias[:, gate, cols], op=ADD)
+                nc.vector.tensor_tensor(out=opened[:], in0=acc[:], in1=bias[:, gate, cols], op=ADD)
                 nc.scalar.activation(out=opened[:], in_=opened[:], func=SIGMOID)
                 input_gate[(col, t)] = opened
             else:
-                result = results.tile([P, N_TILE], F32)
-                nc.vector.tensor_tensor(out=result[:], in0=accs[(col, gate, t)][:], in1=bias[:, gate, cols], op=ADD)
-                sums[(col, t)] = result
+                if first == 0:
+                    sums[(col, t)] = results.tile([P, N_TILE], F32, name="result")
+                nc.vector.tensor_tensor(
+                    out=sums[(col, t)][:, first : first + width], in0=acc[:], in1=bias[:, gate, cols], op=ADD
+                )
 
-        def finish(col, t):
-            cols = slice(N_TILE * col, N_TILE * (col + 1))
+        def finish(col, t, first=0, width=N_TILE):
+            cols = slice(N_TILE * col + first, N_TILE * col + first + width)
+            part_of = slice(first, first + width)
             result = sums[(col, t)]
-            nc.vector.tensor_tensor(out=result[:], in0=result[:], in1=input_gate[(col, t)][:], op=MULT)
-            nc.sync.dma_start(out=out_rows[:, t, cols], in_=result[:])
+            nc.vector.tensor_tensor(
+                out=result[:, part_of], in0=result[:, part_of], in1=input_gate[(col, t)][:, part_of], op=MULT
+            )
+            nc.sync.dma_start(out=out_rows[:, t, cols], in_=result[:, part_of])
 
         for source in range(SOURCES):
             for t in range(ROW_TILES):
@@ -210,8 +217,8 @@ def tile_lstmcell_pa_kernel(
                 if source == SOURCES - 1:
                     add_bias(0, INPUT_GATE, t)
         order = [
-            (0, 1, 0), (0, 1, 1), (0, 1, 2), (1, 0, 0), (0, 1, 3), (1, 0, 1),
-            (1, 1, 0), (1, 0, 2), (1, 1, 1), (1, 0, 3), (1, 1, 2), (1, 1, 3),
+            (0, 1, 0), (0, 1, 1), (0, 1, 2), (0, 1, 3), (1, 0, 0), (1, 0, 1),
+            (1, 1, 0), (1, 1, 1), (1, 0, 2), (1, 1, 2), (1, 0, 3),
         ]
         waiting = None
         for col, gate, t in order:
@@ -223,4 +230,11 @@ def tile_lstmcell_pa_kernel(
                 waiting = None
             if gate != INPUT_GATE:
                 waiting = (col, t)
-        finish(waiting[0], waiting[1])
+        col, t = COL_TILES - 1, ROW_TILES - 1
+        half = N_TILE // 2
+        for first in (0, half):
+            for source in range(SOURCES):
+                passes(col, 1 - INPUT_GATE, t, source, first, half)
+            add_bias(col, 1 - INPUT_GATE, t, first, half)
+        for first in (0, half):
+            finish(col, t, first, half)

@@ -50,10 +50,12 @@ def tile_lstmcell_pa_kernel(
 
     with ExitStack() as ctx:
         keep = ctx.enter_context(tc.tile_pool(name="keep", bufs=1))
-        stage = ctx.enter_context(tc.tile_pool(name="stage", bufs=3))
+        stage = ctx.enter_context(tc.tile_pool(name="stage", bufs=ROW_TILES))
         gates = ctx.enter_context(tc.tile_pool(name="gates", bufs=2 * ROW_TILES))
         results = ctx.enter_context(tc.tile_pool(name="results", bufs=ROW_TILES))
-        psum = ctx.enter_context(tc.psum_pool(name="psum", bufs=8))
+        ring_a = ctx.enter_context(tc.psum_pool(name="ring_a", bufs=4))
+        ring_b = ctx.enter_context(tc.psum_pool(name="ring_b", bufs=4))
+        parts = ctx.enter_context(tc.tile_pool(name="parts", bufs=ROW_TILES))
         ctx.enter_context(tc.manual_schedule())
 
         w_scales = {}
@@ -112,8 +114,8 @@ def tile_lstmcell_pa_kernel(
 
         load_tiles(0)
         load_scales(INPUT_GATE, 0)
-        load_tiles(1)
         load_words(0, INPUT_GATE, 0)
+        load_tiles(1)
         load_scales(INPUT_GATE, 1)
         load_words(0, INPUT_GATE, 1)
         load_scales(1 - INPUT_GATE, 0)
@@ -133,48 +135,60 @@ def tile_lstmcell_pa_kernel(
             for s in range(SOURCES)
         ]
 
-        def turn_and_quantise(source):
-            for t in range(ROW_TILES):
-                pairs = act_raw[source][t][:].bitcast(F32)
-                flipped = psum.tile([P, PASSES, 2, P], F32, tag="bank")
-                for g in range(PASSES):
-                    for u in range(2):
-                        nc.tensor.transpose(
-                            flipped[:, g, u, :],
-                            pairs[:, (K_PASS // 2) * g + u : (K_PASS // 2) * (g + 1) : 2],
-                            ident[:],
-                        )
-                grouped = stage.tile([P, PASSES * P * PACK], BF16, align_bytes=64)
-                nc.scalar.copy(
-                    out=grouped[:].bitcast(F32).rearrange("p (g b u) -> p g b u", g=PASSES, u=2),
-                    in_=flipped[:].rearrange("p g u b -> p g b u"),
-                )
-                nc.vector.quantize_mx(
-                    out=act_codes[source][t][:].bitcast(FP8X4),
-                    scales=act_scales[source][t][:],
-                    in_=grouped[:],
-                )
-
-        turn_and_quantise(0)
-
+        parted = {}
+        grouped = {}
+        spread = {}
         bias = keep.tile([P, GATES, D_OUT], F32)
-        for gate in range(GATES):
-            for col in range(COL_TILES):
-                cols = slice(N_TILE * col, N_TILE * (col + 1))
-                spread = psum.tile([P, N_TILE], F32, tag="bank")
-                nc.tensor.matmul(out=spread[:], lhsT=ones[:], rhs=bias_rows[:, gate, cols], start=True, stop=True)
-                nc.vector.tensor_copy(out=bias[:, gate, cols], in_=spread[:])
 
-        turn_and_quantise(1)
+        def part(source, t):
+            parted[(source, t)] = parts.tile([P, PASSES, 2, P], F32, name="parted")
+            nc.vector.tensor_copy(
+                out=parted[(source, t)][:],
+                in_=act_raw[source][t][:].bitcast(F32).rearrange("p (g j u) -> p g u j", g=PASSES, u=2),
+            )
+
+        def turn(source, t):
+            flipped = ring_a.tile([P, PASSES, 2, P], F32, tag="bank", name="flipped")
+            pairs = act_raw[source][t][:].bitcast(F32)
+            for g in range(PASSES):
+                for u in range(2):
+                    if (source, t) in parted:
+                        words = parted[(source, t)][:, g, u, :]
+                    else:
+                        words = pairs[:, (K_PASS // 2) * g + u : (K_PASS // 2) * (g + 1) : 2]
+                    nc.tensor.transpose(flipped[:, g, u, :], words, ident[:])
+            grouped[(source, t)] = stage.tile([P, PASSES * P * PACK], BF16, name="grouped", align_bytes=64)
+            nc.scalar.copy(
+                out=grouped[(source, t)][:].bitcast(F32).rearrange("p (g b u) -> p g b u", g=PASSES, u=2),
+                in_=flipped[:].rearrange("p g u b -> p g b u"),
+            )
+
+        def quantise(source, t):
+            nc.vector.quantize_mx(
+                out=act_codes[source][t][:].bitcast(FP8X4),
+                scales=act_scales[source][t][:],
+                in_=grouped[(source, t)][:],
+            )
+
+        def spread_bias(gate, col):
+            cols = slice(N_TILE * col, N_TILE * (col + 1))
+            spread[(gate, col)] = ring_a.tile([P, N_TILE], F32, tag="bank", name="spread")
+            nc.tensor.matmul(
+                out=spread[(gate, col)][:], lhsT=ones[:], rhs=bias_rows[:, gate, cols], start=True, stop=True
+            )
+
+        def keep_bias(gate, col):
+            cols = slice(N_TILE * col, N_TILE * (col + 1))
+            nc.vector.tensor_copy(out=bias[:, gate, cols], in_=spread[(gate, col)][:])
 
         accs = {}
         input_gate = {}
         sums = {}
 
-        def passes(col, gate, t, source, first=0, width=N_TILE):
+        def passes(col, gate, t, source, ring=None, first=0, width=N_TILE):
             key = (col, gate, t, first)
             if source == 0:
-                accs[key] = psum.tile([P, width], F32, tag="bank", name="acc")
+                accs[key] = ring.tile([P, width], F32, tag="bank", name="acc")
             cols = slice(N_TILE * col + first, N_TILE * col + first + width)
             for g in range(PASSES):
                 nc.tensor.matmul_mx(
@@ -211,19 +225,38 @@ def tile_lstmcell_pa_kernel(
             )
             nc.sync.dma_start(out=out_rows[:, t, cols], in_=result[:, part_of])
 
-        for source in range(SOURCES):
-            for t in range(ROW_TILES):
-                passes(0, INPUT_GATE, t, source)
-                if source == SOURCES - 1:
-                    add_bias(0, INPUT_GATE, t)
+        for t in range(ROW_TILES):
+            turn(0, t)
+            quantise(0, t)
+        spread_bias(INPUT_GATE, 0)
+        spread_bias(1 - INPUT_GATE, 0)
+        keep_bias(INPUT_GATE, 0)
+        keep_bias(1 - INPUT_GATE, 0)
+        for t in range(ROW_TILES):
+            passes(0, INPUT_GATE, t, 0, ring_b)
+        for t in range(ROW_TILES):
+            part(1, t)
+        for t in range(ROW_TILES):
+            turn(1, t)
+        for t in range(ROW_TILES):
+            quantise(1, t)
+        spread_bias(INPUT_GATE, 1)
+        spread_bias(1 - INPUT_GATE, 1)
+        keep_bias(INPUT_GATE, 1)
+        keep_bias(1 - INPUT_GATE, 1)
+        for t in range(ROW_TILES):
+            passes(0, INPUT_GATE, t, 1)
+            add_bias(0, INPUT_GATE, t)
         order = [
             (0, 1, 0), (0, 1, 1), (0, 1, 2), (0, 1, 3), (1, 0, 0), (1, 0, 1),
             (1, 1, 0), (1, 1, 1), (1, 0, 2), (1, 1, 2), (1, 0, 3),
         ]
+        rings = [ring_a] * 4 + [ring_b] * 4 + [ring_a] * 4 + [ring_b]
         waiting = None
-        for col, gate, t in order:
+        for i in range(len(order)):
+            col, gate, t = order[i]
             for source in range(SOURCES):
-                passes(col, gate, t, source)
+                passes(col, gate, t, source, rings[i])
             add_bias(col, gate, t)
             if waiting is not None:
                 finish(waiting[0], waiting[1])
@@ -232,9 +265,9 @@ def tile_lstmcell_pa_kernel(
                 waiting = (col, t)
         col, t = COL_TILES - 1, ROW_TILES - 1
         half = N_TILE // 2
-        for first in (0, half):
+        for i in range(2):
             for source in range(SOURCES):
-                passes(col, 1 - INPUT_GATE, t, source, first, half)
-            add_bias(col, 1 - INPUT_GATE, t, first, half)
-        for first in (0, half):
-            finish(col, t, first, half)
+                passes(col, 1 - INPUT_GATE, t, source, rings[len(order) + i], half * i, half)
+            add_bias(col, 1 - INPUT_GATE, t, half * i, half)
+        for i in range(2):
+            finish(col, t, half * i, half)

@@ -95,14 +95,16 @@ def tile_lstmcell_pa_kernel(
 
         w_words = {}
 
-        def load_words(col, gate, source):
+        def load_words(col, gate, source, pass_by_pass=False):
             chunk = keep.tile([P, PASSES, N_TILE], U32, name="w%d%d%d" % (col, gate, source), align_bytes=64)
             w_words[(col, gate, source)] = chunk
             view = words_dram[gate][source].rearrange("g p n t -> p g (n t)")
-            nc.sync.dma_start(
-                out=chunk[:].bitcast(I32),
-                in_=view[:, :, PACK * N_TILE * col : PACK * N_TILE * (col + 1)].bitcast(I32),
-            )
+            bytes_of = slice(PACK * N_TILE * col, PACK * N_TILE * (col + 1))
+            if pass_by_pass:
+                for g in range(PASSES):
+                    nc.sync.dma_start(out=chunk[:, g, :].bitcast(I32), in_=view[:, g, bytes_of].bitcast(I32))
+            else:
+                nc.sync.dma_start(out=chunk[:].bitcast(I32), in_=view[:, :, bytes_of].bitcast(I32))
 
         act_raw = [
             [keep.tile([P, D_IN], BF16, name="act_raw%d%d" % (s, t)) for t in range(ROW_TILES)]
@@ -114,7 +116,7 @@ def tile_lstmcell_pa_kernel(
 
         load_tiles(0)
         load_scales(INPUT_GATE, 0)
-        load_words(0, INPUT_GATE, 0)
+        load_words(0, INPUT_GATE, 0, pass_by_pass=True)
         load_tiles(1)
         load_scales(INPUT_GATE, 1)
         load_words(0, INPUT_GATE, 1)
@@ -185,12 +187,12 @@ def tile_lstmcell_pa_kernel(
         input_gate = {}
         sums = {}
 
-        def passes(col, gate, t, source, ring=None, first=0, width=N_TILE):
+        def passes(col, gate, t, source, ring=None, first=0, width=N_TILE, which=(0, 1)):
             key = (col, gate, t, first)
-            if source == 0:
+            if source == 0 and which[0] == 0:
                 accs[key] = ring.tile([P, width], F32, tag="bank", name="acc")
             cols = slice(N_TILE * col + first, N_TILE * col + first + width)
-            for g in range(PASSES):
+            for g in which:
                 nc.tensor.matmul_mx(
                     out=accs[key][:],
                     lhsT=act_codes[source][t][:, P * g : P * (g + 1)].bitcast(FP8X4),
@@ -232,8 +234,9 @@ def tile_lstmcell_pa_kernel(
         spread_bias(1 - INPUT_GATE, 0)
         keep_bias(INPUT_GATE, 0)
         keep_bias(1 - INPUT_GATE, 0)
-        for t in range(ROW_TILES):
-            passes(0, INPUT_GATE, t, 0, ring_b)
+        for g in range(PASSES):
+            for t in range(ROW_TILES):
+                passes(0, INPUT_GATE, t, 0, ring_b, which=(g,))
         for t in range(ROW_TILES):
             part(1, t)
         for t in range(ROW_TILES):

@@ -62,7 +62,7 @@ def tile_lstmcell_pa_kernel(
         for gate in range(GATES):
             for source in range(SOURCES):
                 w_scales[(gate, source)] = keep.tile(
-                    [P, D_OUT], U8, name="w_scales%d%d" % (gate, source), align_bytes=64
+                    [P, D_OUT], U8, name="w_scales%d%d" % (gate, source), align_bytes=256
                 )
         nc.vector.memset(w_scales[(INPUT_GATE, 0)][:].bitcast(I32), 0)
         bias_rows = keep.tile([P, GATES, D_OUT], BF16)
@@ -96,7 +96,7 @@ def tile_lstmcell_pa_kernel(
         w_words = {}
 
         def load_words(col, gate, source, pass_by_pass=False):
-            chunk = keep.tile([P, PASSES, N_TILE], U32, name="w%d%d%d" % (col, gate, source), align_bytes=64)
+            chunk = keep.tile([P, PASSES, N_TILE], U32, name="w%d%d%d" % (col, gate, source), align_bytes=256)
             w_words[(col, gate, source)] = chunk
             view = words_dram[gate][source].rearrange("g p n t -> p g (n t)")
             bytes_of = slice(PACK * N_TILE * col, PACK * N_TILE * (col + 1))
@@ -129,11 +129,11 @@ def tile_lstmcell_pa_kernel(
                 load_words(1, gate, source)
 
         act_codes = [
-            [keep.tile([P, PASSES * P], U32, name="codes%d%d" % (s, t), align_bytes=64) for t in range(ROW_TILES)]
+            [keep.tile([P, PASSES * P], U32, name="codes%d%d" % (s, t), align_bytes=256) for t in range(ROW_TILES)]
             for s in range(SOURCES)
         ]
         act_scales = [
-            [keep.tile([P, PASSES * P], U8, name="scales%d%d" % (s, t), align_bytes=64) for t in range(ROW_TILES)]
+            [keep.tile([P, PASSES * P], U8, name="scales%d%d" % (s, t), align_bytes=256) for t in range(ROW_TILES)]
             for s in range(SOURCES)
         ]
 
@@ -159,7 +159,7 @@ def tile_lstmcell_pa_kernel(
                     else:
                         words = pairs[:, (K_PASS // 2) * g + u : (K_PASS // 2) * (g + 1) : 2]
                     nc.tensor.transpose(flipped[:, g, u, :], words, ident[:])
-            grouped[(source, t)] = stage.tile([P, PASSES * P * PACK], BF16, name="grouped", align_bytes=64)
+            grouped[(source, t)] = stage.tile([P, PASSES * P * PACK], BF16, name="grouped", align_bytes=256)
             nc.scalar.copy(
                 out=grouped[(source, t)][:].bitcast(F32).rearrange("p (g b u) -> p g b u", g=PASSES, u=2),
                 in_=flipped[:].rearrange("p g u b -> p g b u"),

@@ -65,17 +65,17 @@ def tile_lstmcell_pa_kernel(
                     [P, D_OUT], U8, name="w_scales%d%d" % (gate, source), align_bytes=256
                 )
         nc.vector.memset(w_scales[(INPUT_GATE, 0)][:].bitcast(I32), 0)
-        bias_rows = keep.tile([P, GATES, D_OUT], BF16)
+        bias_rows = keep.tile([P, GATES, D_OUT], BF16, align_bytes=256)
         nc.vector.memset(bias_rows[:], 0.0)
         nc.vector.memset(w_scales[(INPUT_GATE, 1)][:].bitcast(I32), 0)
         nc.vector.memset(w_scales[(1 - INPUT_GATE, 0)][:].bitcast(I32), 0)
         nc.vector.memset(w_scales[(1 - INPUT_GATE, 1)][:].bitcast(I32), 0)
-        ones = keep.tile([P, P], BF16)
+        ones = keep.tile([P, P], BF16, align_bytes=256)
         nc.vector.memset(ones[:], 1.0)
         warm = keep.tile([P, 1], F32)
         nc.gpsimd.memset(warm[:], 0.0)
         nc.scalar.activation(out=warm[:], in_=warm[:], func=SIGMOID)
-        ident = keep.tile([P, P], F32)
+        ident = keep.tile([P, P], F32, align_bytes=256)
         make_identity(nc, ident[:])
         for gate in range(GATES):
             for source in range(SOURCES):
@@ -107,7 +107,7 @@ def tile_lstmcell_pa_kernel(
                 nc.sync.dma_start(out=chunk[:].bitcast(I32), in_=view[:, :, bytes_of].bitcast(I32))
 
         act_raw = [
-            [keep.tile([P, D_IN], BF16, name="act_raw%d%d" % (s, t)) for t in range(ROW_TILES)]
+            [keep.tile([P, D_IN], BF16, name="act_raw%d%d" % (s, t), align_bytes=256) for t in range(ROW_TILES)]
             for s in range(SOURCES)
         ]
         def load_tiles(source):
@@ -143,7 +143,7 @@ def tile_lstmcell_pa_kernel(
         bias = keep.tile([P, GATES, D_OUT], F32)
 
         def part(source, t):
-            parted[(source, t)] = parts.tile([P, PASSES, 2, P], F32, name="parted")
+            parted[(source, t)] = parts.tile([P, PASSES, 2, P], F32, name="parted", align_bytes=256)
             nc.vector.tensor_copy(
                 out=parted[(source, t)][:],
                 in_=act_raw[source][t][:].bitcast(F32).rearrange("p (g j u) -> p g u j", g=PASSES, u=2),

from contextlib import ExitStack

import concourse.mybir as mybir
from concourse.masks import make_identity

F32 = mybir.dt.float32
BF16 = mybir.dt.bfloat16
I32 = mybir.dt.int32
U32 = mybir.dt.uint32
U8 = mybir.dt.uint8
FP8X4 = mybir.dt.float8_e4m3fn_x4
ADD = mybir.AluOpType.add
MULT = mybir.AluOpType.mult
SIGMOID = mybir.ActivationFunctionType.Sigmoid

P = 128
PACK = 4
K_PASS = P * PACK
BATCH = 512
D_IN = 1024
D_OUT = 1024
ROW_TILES = BATCH // P
PASSES = D_IN // K_PASS
N_TILE = 512
COL_TILES = D_OUT // N_TILE
QUADRANTS = 4
ROWS_PER_QUADRANT = 4
SOURCES = 2
GATES = 2
INPUT_GATE = 0

FLOPS = 2 * BATCH * (SOURCES * D_IN) * (GATES * D_OUT)


def tile_lstmcell_pa_kernel(
    tc,
    incoming, h,
    W_i_words, W_i_scales, b_W_i,
    W_c_words, W_c_scales, b_W_c,
    U_i_words, U_i_scales, b_U_i,
    U_c_words, U_c_scales, b_U_c,
    out,
):
    nc = tc.nc
    words_dram = [[W_i_words, U_i_words], [W_c_words, U_c_words]]
    scales_dram = [[W_i_scales, U_i_scales], [W_c_scales, U_c_scales]]
    bias_dram = [[b_W_i, b_U_i], [b_W_c, b_U_c]]
    acts_dram = [a.rearrange("(p t) k -> p t k", t=ROW_TILES) for a in (incoming, h)]
    out_rows = out.rearrange("(p t) n -> p t n", t=ROW_TILES)

    with ExitStack() as ctx:
        keep = ctx.enter_context(tc.tile_pool(name="keep", bufs=1))
        stage = ctx.enter_context(tc.tile_pool(name="stage", bufs=ROW_TILES))
        gates = ctx.enter_context(tc.tile_pool(name="gates", bufs=2 * ROW_TILES))
        results = ctx.enter_context(tc.tile_pool(name="results", bufs=ROW_TILES))
        ring_a = ctx.enter_context(tc.psum_pool(name="ring_a", bufs=4))
        ring_b = ctx.enter_context(tc.psum_pool(name="ring_b", bufs=4))
        parts = ctx.enter_context(tc.tile_pool(name="parts", bufs=ROW_TILES))
        ctx.enter_context(tc.manual_schedule())

        w_scales = {}
        for gate in range(GATES):
            for source in range(SOURCES):
                w_scales[(gate, source)] = keep.tile(
                    [P, D_OUT], U8, name="w_scales%d%d" % (gate, source), align_bytes=256
                )
        nc.vector.memset(w_scales[(INPUT_GATE, 0)][:].bitcast(I32), 0)
        bias_rows = keep.tile([P, GATES, D_OUT], BF16, align_bytes=256)
        nc.vector.memset(bias_rows[:], 0.0)
        nc.vector.memset(w_scales[(INPUT_GATE, 1)][:].bitcast(I32), 0)
        nc.vector.memset(w_scales[(1 - INPUT_GATE, 0)][:].bitcast(I32), 0)
        nc.vector.memset(w_scales[(1 - INPUT_GATE, 1)][:].bitcast(I32), 0)
        ones = keep.tile([P, P], BF16, align_bytes=256)
        nc.vector.memset(ones[:], 1.0)
        warm = keep.tile([P, 1], F32)
        nc.gpsimd.memset(warm[:], 0.0)
        nc.scalar.activation(out=warm[:], in_=warm[:], func=SIGMOID)
        ident = keep.tile([P, P], F32, align_bytes=256)
        make_identity(nc, ident[:])
        for gate in range(GATES):
            for source in range(SOURCES):
                nc.scalar.dma_start(
                    out=bias_rows[source : source + 1, gate, :],
                    in_=bias_dram[gate][source].rearrange("(o n) -> o n", o=1),
                )

        def load_scales(gate, source):
            for quadrant in range(QUADRANTS):
                rows = slice(ROWS_PER_QUADRANT * quadrant, ROWS_PER_QUADRANT * (quadrant + 1))
                first = 32 * quadrant
                nc.sync.dma_start(
                    out=w_scales[(gate, source)][first : first + ROWS_PER_QUADRANT * PASSES, :].bitcast(I32),
                    in_=scales_dram[gate][source][:, rows, :].bitcast(I32),
                )

        w_words = {}

        def load_words(col, gate, source, pass_by_pass=False):
            chunk = keep.tile([P, PASSES, N_TILE], U32, name="w%d%d%d" % (col, gate, source), align_bytes=256)
            w_words[(col, gate, source)] = chunk
            view = words_dram[gate][source].rearrange("g p n t -> p g (n t)")
            bytes_of = slice(PACK * N_TILE * col, PACK * N_TILE * (col + 1))
            if pass_by_pass:
                for g in range(PASSES):
                    nc.sync.dma_start(out=chunk[:, g, :].bitcast(I32), in_=view[:, g, bytes_of].bitcast(I32))
            else:
                nc.sync.dma_start(out=chunk[:].bitcast(I32), in_=view[:, :, bytes_of].bitcast(I32))

        act_raw = [
            [keep.tile([P, D_IN], BF16, name="act_raw%d%d" % (s, t), align_bytes=256) for t in range(ROW_TILES)]
            for s in range(SOURCES)
        ]
        def load_tiles(source):
            for t in range(ROW_TILES):
                nc.sync.dma_start(out=act_raw[source][t][:], in_=acts_dram[source][:, t, :])

        load_tiles(0)
        load_scales(INPUT_GATE, 0)
        load_words(0, INPUT_GATE, 0, pass_by_pass=True)
        load_tiles(1)
        load_scales(INPUT_GATE, 1)
        load_words(0, INPUT_GATE, 1)
        load_scales(1 - INPUT_GATE, 0)
        load_words(0, 1 - INPUT_GATE, 0)
        load_scales(1 - INPUT_GATE, 1)
        load_words(0, 1 - INPUT_GATE, 1)
        for gate in range(GATES):
            for source in range(SOURCES):
                load_words(1, gate, source)

        act_codes = [
            [keep.tile([P, PASSES * P], U32, name="codes%d%d" % (s, t), align_bytes=256) for t in range(ROW_TILES)]
            for s in range(SOURCES)
        ]
        act_scales = [
            [keep.tile([P, PASSES * P], U8, name="scales%d%d" % (s, t), align_bytes=256) for t in range(ROW_TILES)]
            for s in range(SOURCES)
        ]

        parted = {}
        grouped = {}
        spread = {}
        bias = keep.tile([P, GATES, D_OUT], F32)

        def part(source, t):
            parted[(source, t)] = parts.tile([P, PASSES, 2, P], F32, name="parted", align_bytes=256)
            nc.vector.tensor_copy(
                out=parted[(source, t)][:],
                in_=act_raw[source][t][:].bitcast(F32).rearrange("p (g j u) -> p g u j", g=PASSES, u=2),
            )

        def turn(source, t):
            flipped = ring_a.tile([P, PASSES, 2, P], F32, tag="bank", name="flipped")
            pairs = act_raw[source][t][:].bitcast(F32)
            for g in range(PASSES):
                for u in range(2):
                    if (source, t) in parted:
                        words = parted[(source, t)][:, g, u, :]
                    else:
                        words = pairs[:, (K_PASS // 2) * g + u : (K_PASS // 2) * (g + 1) : 2]
                    nc.tensor.transpose(flipped[:, g, u, :], words, ident[:])
            grouped[(source, t)] = stage.tile([P, PASSES * P * PACK], BF16, name="grouped", align_bytes=256)
            nc.scalar.copy(
                out=grouped[(source, t)][:].bitcast(F32).rearrange("p (g b u) -> p g b u", g=PASSES, u=2),
                in_=flipped[:].rearrange("p g u b -> p g b u"),
            )

        def quantise(source, t):
            nc.vector.quantize_mx(
                out=act_codes[source][t][:].bitcast(FP8X4),
                scales=act_scales[source][t][:],
                in_=grouped[(source, t)][:],
            )

        def spread_bias(gate, col):
            cols = slice(N_TILE * col, N_TILE * (col + 1))
            spread[(gate, col)] = ring_a.tile([P, N_TILE], F32, tag="bank", name="spread")
            nc.tensor.matmul(
                out=spread[(gate, col)][:], lhsT=ones[:], rhs=bias_rows[:, gate, cols], start=True, stop=True
            )

        def keep_bias(gate, col):
            cols = slice(N_TILE * col, N_TILE * (col + 1))
            nc.vector.tensor_copy(out=bias[:, gate, cols], in_=spread[(gate, col)][:])

        accs = {}
        input_gate = {}
        sums = {}

        def passes(col, gate, t, source, ring=None, first=0, width=N_TILE, which=(0, 1)):
            key = (col, gate, t, first)
            if source == 0 and which[0] == 0:
                accs[key] = ring.tile([P, width], F32, tag="bank", name="acc")
            cols = slice(N_TILE * col + first, N_TILE * col + first + width)
            for g in which:
                nc.tensor.matmul_mx(
                    out=accs[key][:],
                    lhsT=act_codes[source][t][:, P * g : P * (g + 1)].bitcast(FP8X4),
                    lhsT_scale=act_scales[source][t][:, P * g : P * (g + 1)],
                    rhs=w_words[(col, gate, source)][:, g, first : first + width].bitcast(FP8X4),
                    rhs_scale=w_scales[(gate, source)][ROWS_PER_QUADRANT * g : P, cols],
                    start=(source == 0 and g == 0),
                    stop=(source == SOURCES - 1 and g == PASSES - 1),
                )

        def add_bias(col, gate, t, first=0, width=N_TILE):
            cols = slice(N_TILE * col + first, N_TILE * col + first + width)
            acc = accs[(col, gate, t, first)]
            if gate == INPUT_GATE:
                opened = gates.tile([P, N_TILE], F32)
                nc.vector.tensor_tensor(out=opened[:], in0=acc[:], in1=bias[:, gate, cols], op=ADD)
                nc.scalar.activation(out=opened[:], in_=opened[:], func=SIGMOID)
                input_gate[(col, t)] = opened
            else:
                if first == 0:
                    sums[(col, t)] = results.tile([P, N_TILE], F32, name="result")
                nc.vector.tensor_tensor(
                    out=sums[(col, t)][:, first : first + width], in0=acc[:], in1=bias[:, gate, cols], op=ADD
                )

        def finish(col, t, first=0, width=N_TILE):
            cols = slice(N_TILE * col + first, N_TILE * col + first + width)
            part_of = slice(first, first + width)
            result = sums[(col, t)]
            nc.vector.tensor_tensor(
                out=result[:, part_of], in0=result[:, part_of], in1=input_gate[(col, t)][:, part_of], op=MULT
            )
            nc.sync.dma_start(out=out_rows[:, t, cols], in_=result[:, part_of])

        for t in range(ROW_TILES):
            turn(0, t)
            quantise(0, t)
        spread_bias(INPUT_GATE, 0)
        spread_bias(1 - INPUT_GATE, 0)
        keep_bias(INPUT_GATE, 0)
        keep_bias(1 - INPUT_GATE, 0)
        for g in range(PASSES):
            for t in range(ROW_TILES):
                passes(0, INPUT_GATE, t, 0, ring_b, which=(g,))
        for t in range(ROW_TILES):
            part(1, t)
        for t in range(ROW_TILES):
            turn(1, t)
        for t in range(ROW_TILES):
            quantise(1, t)
        spread_bias(INPUT_GATE, 1)
        spread_bias(1 - INPUT_GATE, 1)
        keep_bias(INPUT_GATE, 1)
        keep_bias(1 - INPUT_GATE, 1)
        for t in range(ROW_TILES):
            passes(0, INPUT_GATE, t, 1)
            add_bias(0, INPUT_GATE, t)
        order = [
            (0, 1, 0), (0, 1, 1), (0, 1, 2), (0, 1, 3), (1, 0, 0), (1, 0, 1),
            (1, 1, 0), (1, 1, 1), (1, 0, 2), (1, 1, 2), (1, 0, 3),
        ]
        rings = [ring_a] * 4 + [ring_b] * 4 + [ring_a] * 4 + [ring_b]
        waiting = None
        for i in range(len(order)):
            col, gate, t = order[i]
            for source in range(SOURCES):
                passes(col, gate, t, source, rings[i])
            add_bias(col, gate, t)
            if waiting is not None:
                finish(waiting[0], waiting[1])
                waiting = None
            if gate != INPUT_GATE:
                waiting = (col, t)
        col, t = COL_TILES - 1, ROW_TILES - 1
        half = N_TILE // 2
        for i in range(2):
            for source in range(SOURCES):
                passes(col, 1 - INPUT_GATE, t, source, rings[len(order) + i], half * i, half)
            add_bias(col, 1 - INPUT_GATE, t, half * i, half)
        for i in range(2):
            finish(col, t, half * i, half)
